import numpy as np
import ml_dtypes


def mxq(x, axis, fmt="e4m3"):
    dtype, down = {"e4m3": (ml_dtypes.float8_e4m3fn, 7), "e5m2": (ml_dtypes.float8_e5m2, 14)}[fmt]
    v = np.moveaxis(np.asarray(x, np.float32).astype(ml_dtypes.bfloat16).astype(np.float64), axis, -1)
    blocks = v.reshape(v.shape[:-1] + (-1, 32))
    amax = np.abs(blocks).max(-1, keepdims=True)
    byte = np.maximum(np.where(amax > 0, np.frexp(amax)[1] - 1 + 127, 0) - down, 1)
    scale = np.exp2(byte - 127.0)
    codes = (blocks / scale).astype(np.float32).astype(dtype).astype(np.float64)
    return np.moveaxis((codes * scale).reshape(v.shape), -1, axis)


WIDE = False


def mx_kscale(k):
    if not WIDE:
        return np.ones(k)
    levels = np.array([10, -10, 5, -5, 0])
    a = np.random.permutation(np.resize(levels, k // 512 * 4)).reshape(k // 512, 4)
    idx = np.arange(k)
    return np.exp2(a[idx // 512, idx % 128 // 32])


BF16 = ml_dtypes.bfloat16


def bf(x):
    return np.asarray(x, np.float32).astype(BF16)


def f64(x):
    return np.asarray(x).astype(np.float64)


B, N, F, D = 8, 1024, 128, 256


def normalize_adjacency(adj):
    d = np.sum(adj, axis=-1)
    with np.errstate(divide="ignore"):
        d_sqrt_inv = np.power(d, -0.5)
    d_sqrt_inv = np.where(np.isinf(d_sqrt_inv), 0.0, d_sqrt_inv)
    return d_sqrt_inv[..., :, None] * adj * d_sqrt_inv[..., None, :]


def setup_inputs():
    s = mx_kscale(N)
    g = s.mean()
    return {"inputs": bf(np.random.standard_normal((B, N, F)) * (g / s)[:, None]),
            "adj": bf(np.random.uniform(size=(B, N, N)) * s),
            "W_kernel": bf(np.random.standard_normal((F, D)) * 0.2 * np.sqrt(N / F)),
            "W_bias": bf(np.random.standard_normal(D) * 0.2)}


def reference(inputs, adj, W_kernel, W_bias):
    adj_norm = normalize_adjacency(f64(adj))
    feats = f64(inputs) @ f64(W_kernel) + f64(W_bias)
    out = mxq(adj_norm, 2, "e4m3") @ mxq(feats, 1, "e4m3")
    return np.maximum(out, 0.0)

@@ -1,0 +1,349 @@
+from contextlib import ExitStack
+
+import concourse.mybir as mybir
+from concourse.masks import make_identity
+
+F32 = mybir.dt.float32
+BF16 = mybir.dt.bfloat16
+U32 = mybir.dt.uint32
+U8 = mybir.dt.uint8
+FP8X4 = mybir.dt.float8_e4m3fn_x4
+ALU = mybir.AluOpType
+ACT = mybir.ActivationFunctionType
+
+B, N, F, D = 8, 1024, 128, 256
+P = 128
+FLOPS = 2 * B * N * N * D + 2 * B * N * F * D
+
+PIN = True
+LW = 3
+XF0 = -24
+DXF = 8
+LFM = 3
+DF = 2
+LFB = 2
+LQF = 0.5
+DMX = 2
+LRL = 2
+LRS = 20
+DRS = 0.8
+LRV = 4
+LRC = 0.2
+DRP = 1
+VH = {}
+VHD = []
+RPW = {}
+RPWD = "GGGGGGGG"
+RG_BUFS = 3
+W_BUFS = 3
+F_BUFS = 1
+X_BUFS = 2
+
+
+def tile_gcn_t_kernel(tc, inputs, adj, W_kernel, W_bias, out):
+    nc = tc.nc
+    with ExitStack() as ctx:
+        if PIN:
+            ctx.enter_context(tc.manual_schedule())
+        const = ctx.enter_context(tc.tile_pool(name="const", bufs=1))
+        apool = ctx.enter_context(tc.tile_pool(name="apool", bufs=4))
+        rpool = ctx.enter_context(tc.tile_pool(name="rpool", bufs=RG_BUFS))
+        work = ctx.enter_context(tc.tile_pool(name="work", bufs=2))
+        small = ctx.enter_context(tc.tile_pool(name="small", bufs=3))
+        keep = ctx.enter_context(tc.tile_pool(name="keep", bufs=B))
+        opool = ctx.enter_context(tc.tile_pool(name="opool", bufs=4))
+        psum = ctx.enter_context(tc.psum_pool(name="psum", bufs=1))
+
+        warm = const.tile([P, 1], F32, name="warm")
+        nc.vector.memset(warm[:], 1.0)
+        nc.scalar.activation(out=warm[:], in_=warm[:], func=ACT.Sqrt)
+        ident_b = const.tile([P, P], BF16, name="ident_b")
+        make_identity(nc, ident_b[:])
+        ident_f = const.tile([P, P], F32, name="ident_f")
+        make_identity(nc, ident_f[:])
+        w_sb = const.tile([P, D], BF16, name="w_sb")
+        nc.sync.dma_start(out=w_sb[:], in_=W_kernel)
+        bias_bc = const.tile([P, D], BF16, name="bias_bc")
+        nc.sync.dma_start(out=bias_bc[:], in_=W_bias.partition_broadcast(P))
+        x_sb = const.tile([P, B, 8, F], BF16, name="x_sb")
+        xv = inputs.rearrange("b (q p e) f -> p b q (e f)", q=4, p=P, e=2)
+        junk = const.tile([P, N], BF16, name="junk")
+        junkv = const.tile([P, N // 2], F32, name="junkv") if (VH or VHD) else None
+
+        st = {}
+        plan = []
+
+        def at(x, fn):
+            plan.append((x, len(plan), fn))
+
+        def load_x(i):
+            nc.sync.dma_start(
+                out=x_sb[:, 2 * i : 2 * i + 2].rearrange("p b (q e) f -> p b q (e f)", q=4, e=2),
+                in_=xv[:, 2 * i : 2 * i + 2],
+            )
+
+        def load_a(b, q):
+            if q == 0:
+                a_new = apool.tile([P, 8, N], BF16, name="a_sb")
+                st[("a", b)] = a_new
+            av = adj[b].rearrange("(q p e) m -> p q e m", q=4, p=P, e=2)
+            nc.sync.dma_start(out=st[("a", b)][:, 2 * q : 2 * q + 2, :], in_=av[:, q])
+
+        def x_transpose(b):
+            xtp = psum.tile([P, 8, P], BF16, name="xtp", tag="x", bufs=X_BUFS)
+            for j in range(8):
+                nc.tensor.transpose(xtp[:, j, :], x_sb[:, b, j, :], ident_b[:])
+            st[("xtp", b)] = xtp
+
+        def x_copy(b):
+            xt = work.tile([P, 8, P], BF16, name="xt")
+            nc.scalar.copy(out=xt[:], in_=st[("xtp", b)][:])
+            st[("xt", b)] = xt
+
+        def f_matmul(b, i):
+            g, h = divmod(i, 2)
+            fp = psum.tile([P, 4, P], F32, name="fp", tag="f", bufs=F_BUFS)
+            for t in range(4):
+                nc.tensor.matmul(
+                    fp[:, t, :],
+                    lhsT=st[("xt", b)][:, 4 * g + t, :],
+                    rhs=w_sb[:, h * P : (h + 1) * P],
+                    start=True,
+                    stop=True,
+                )
+            st[("fp", b, i)] = fp
+
+        def f_bias(b, i):
+            g, h = divmod(i, 2)
+            if i == 0:
+                fg_new = work.tile([P, 2, D, 4], BF16, name="fg", align_bytes=64)
+                st[("fg", b)] = fg_new
+            nc.vector.tensor_tensor(
+                out=st[("fg", b)][:, g, h * P : (h + 1) * P, :],
+                in0=st[("fp", b, i)][:].rearrange("p t d -> p d t"),
+                in1=bias_bc[:, h * P : (h + 1) * P].unsqueeze(2).to_broadcast([P, P, 4]),
+                op=ALU.add,
+            )
+
+        def f_quant(b):
+            fc = keep.tile([P, 2 * D], U32, name="fc", align_bytes=64)
+            fs = keep.tile([P, 2 * D], U8, name="fs", align_bytes=64)
+            nc.vector.quantize_mx(
+                out=fc[:].bitcast(FP8X4),
+                scales=fs[:],
+                in_=st[("fg", b)][:].rearrange("p g d t -> p (g d t)"),
+            )
+            st[("fc", b)] = (fc, fs)
+
+        def vh_of(b):
+            return VH.get(b, VHD)
+
+        def rowsum(b, j):
+            a_sb = st[("a", b)]
+            if j == 0:
+                deg_new = small.tile([P, 8], F32, name="deg")
+                st[("deg", b)] = deg_new
+                if vh_of(b):
+                    degv_new = small.tile([P, 8], F32, name="degv")
+                    st[("degv", b)] = degv_new
+            if j in vh_of(b):
+                nc.vector.scalar_tensor_tensor(
+                    out=junkv[:],
+                    in0=a_sb[:, j, 0 : N // 2],
+                    scalar=1.0,
+                    in1=a_sb[:, j, N // 2 : N],
+                    op0=ALU.mult,
+                    op1=ALU.add,
+                    accum_out=st[("degv", b)][:, j : j + 1],
+                )
+            else:
+                nc.scalar.activation(
+                    out=junk[:],
+                    in_=a_sb[:, j, :],
+                    func=ACT.Copy,
+                    accum_out=st[("deg", b)][:, j : j + 1],
+                )
+
+        def runs(b):
+            res = []
+            for j in range(8):
+                key = "degv" if j in vh_of(b) else "deg"
+                if res and res[-1][0] == key:
+                    res[-1][2] = j + 1
+                else:
+                    res.append([key, j, j + 1])
+            return res
+
+        def root(b):
+            rt = small.tile([P, 8], F32, name="rt")
+            for key, j0, j1 in runs(b):
+                nc.scalar.activation(out=rt[:, j0:j1], in_=st[(key, b)][:, j0:j1], func=ACT.Sqrt)
+            st[("rt", b)] = rt
+
+        def rvec(b):
+            rtc = small.tile([P, 8], F32, name="rtc")
+            nc.vector.tensor_scalar_max(out=rtc[:], in0=st[("rt", b)][:], scalar1=1e-30)
+            inv = small.tile([P, 8], F32, name="inv")
+            nc.vector.reciprocal(out=inv[:], in_=rtc[:])
+            r = small.tile([P, 8], F32, name="r")
+            for key, j0, j1 in runs(b):
+                nc.vector.scalar_tensor_tensor(
+                    out=r[:, j0:j1],
+                    in0=st[(key, b)][:, j0:j1],
+                    scalar=0.0,
+                    in1=inv[:, j0:j1],
+                    op0=ALU.is_gt,
+                    op1=ALU.mult,
+                )
+            st[("r", b)] = r
+
+        def r_transpose(b, hh):
+            rnp = psum.tile([P, 4, P], F32, name="rnp", tag="x", bufs=X_BUFS)
+            r = st[("r", b)]
+            for jj in range(4):
+                j = 4 * hh + jj
+                nc.tensor.transpose(rnp[:, jj, :], r[:, j : j + 1].to_broadcast([P, P]), ident_f[:])
+            st[("rnp", b, hh)] = rnp
+
+        def r_copy(b, hh):
+            if hh == 0:
+                rn_new = work.tile([P, N], F32, name="rn")
+                st[("rn", b)] = rn_new
+            nc.scalar.copy(
+                out=st[("rn", b)][:, hh * 512 : (hh + 1) * 512],
+                in_=st[("rnp", b, hh)][:].rearrange("p a c -> p (a c)"),
+            )
+
+        def r_plane(b, g, t):
+            if t == 0:
+                rg_new = rpool.tile([P, 4, N], F32, name="rg")
+                st[("rg", b, g)] = rg_new
+            who = RPW.get(b, RPWD)[4 * g + t]
+            dst = st[("rg", b, g)][:, t, :]
+            src = st[("rn", b)][:]
+            sc = st[("r", b)][:, 4 * g + t : 4 * g + t + 1]
+            if who == "G":
+                nc.gpsimd.tensor_scalar(
+                    out=dst, in0=src, scalar1=sc, scalar2=0.0, op0=ALU.mult, op1=ALU.add
+                )
+            elif who == "V":
+                nc.vector.tensor_scalar_mul(out=dst, in0=src, scalar1=sc)
+            else:
+                nc.scalar.activation(out=dst, in_=src, func=ACT.Copy, scale=sc)
+
+        def a_transpose(b, s):
+            g, nb = divmod(s, 4)
+            a_sb = st[("a", b)]
+            tp = psum.tile([P, 512], F32, name="tp", tag="w", bufs=W_BUFS)
+            for u in range(2):
+                for jj in range(2):
+                    j = 2 * nb + jj
+                    c0 = 256 * g + 128 * u
+                    nc.tensor.transpose(
+                        tp[:, u * 256 + jj * P : u * 256 + (jj + 1) * P],
+                        a_sb[:, j, :].bitcast(F32)[:, c0 : c0 + P],
+                        ident_f[:],
+                    )
+            st[("tp", b, s)] = tp
+
+        def a_scale(b, s):
+            g, nb = divmod(s, 4)
+            if nb == 0:
+                gq_new = work.tile([P, N, 4], BF16, name="gq", align_bytes=64)
+                st[("gq", b, g)] = gq_new
+            nc.vector.tensor_tensor(
+                out=st[("gq", b, g)][:, nb * 256 : (nb + 1) * 256, :].rearrange(
+                    "p n (u e) -> p n u e", u=2, e=2
+                ),
+                in0=st[("tp", b, s)][:]
+                .bitcast(BF16)
+                .rearrange("p (u n e) -> p n u e", u=2, n=256, e=2),
+                in1=st[("rg", b, g)][:, :, nb * 256 : (nb + 1) * 256].rearrange(
+                    "p (u e) n -> p n u e", u=2, e=2
+                ),
+                op=ALU.mult,
+            )
+
+        def a_quant(b, g):
+            if g == 0:
+                ac_new = work.tile([P, 2 * N], U32, name="ac", align_bytes=64)
+                asc_new = work.tile([P, 2 * N], U8, name="asc", align_bytes=64)
+                st[("ac", b)] = (ac_new, asc_new)
+            ac, asc = st[("ac", b)]
+            nc.vector.quantize_mx(
+                out=ac[:, g * N : (g + 1) * N].bitcast(FP8X4),
+                scales=asc[:, g * N : (g + 1) * N],
+                in_=st[("gq", b, g)][:].rearrange("p n t -> p (n t)"),
+            )
+
+        def mx(b, q):
+            ac, asc = st[("ac", b)]
+            fc, fs = st[("fc", b)]
+            op = psum.tile([P, 2, D], F32, name="op", tag="o", bufs=2)
+            for e in range(2):
+                j = 2 * q + e
+                for g in range(2):
+                    c0 = g * N + j * P
+                    nc.tensor.matmul_mx(
+                        out=op[:, e, :],
+                        lhsT=ac[:, c0 : c0 + P].bitcast(FP8X4),
+                        lhsT_scale=asc[:, c0 : c0 + P],
+                        rhs=fc[:, g * D : (g + 1) * D].bitcast(FP8X4),
+                        rhs_scale=fs[:, g * D : (g + 1) * D],
+                        start=(g == 0),
+                        stop=(g == 1),
+                    )
+            st[("op", b, q)] = op
+
+        def relu_store(b, q):
+            ov = out[b].rearrange("(q p e) d -> p q e d", q=4, p=P, e=2)
+            o_sb = opool.tile([P, 2, D], F32, name="o_sb")
+            nc.scalar.activation(out=o_sb[:], in_=st[("op", b, q)][:], func=ACT.Relu)
+            nc.scalar.dma_start(out=ov[:, q], in_=o_sb[:])
+
+        lx = -1000.0
+        for kind, i in (("x", 0), ("a", 0), ("x", 1), ("a", 1), ("x", 2), ("x", 3), ("a", 2), ("a", 3)):
+            if kind == "x":
+                lx += 0.01
+                at(lx, lambda i=i: load_x(i))
+            else:
+                for q in range(4):
+                    lx += 0.01
+                    at(lx, lambda i=i, q=q: load_a(i, q))
+        for b in range(4, B):
+            for q in range(4):
+                at(8 * (b - 4) + 7 - LW + 0.3 + q * 0.01, lambda b=b, q=q: load_a(b, q))
+        for b in range(B):
+            for s in range(8):
+                at(8 * b + s - LW - 0.5, lambda b=b, s=s: a_transpose(b, s))
+                at(8 * b + s, lambda b=b, s=s: a_scale(b, s))
+            at(8 * b + 4.5, lambda b=b: a_quant(b, 0))
+            at(8 * b + 8.5, lambda b=b: a_quant(b, 1))
+            x0 = XF0 + b * DXF
+            at(x0, lambda b=b: x_transpose(b))
+            at(x0 + 0.05, lambda b=b: x_copy(b))
+            for i in range(4):
+                at(x0 + LFM + i * DF, lambda b=b, i=i: f_matmul(b, i))
+                at(x0 + LFM + i * DF + LFB, lambda b=b, i=i: f_bias(b, i))
+            at(x0 + LFM + 3 * DF + LFB + LQF, lambda b=b: f_quant(b))
+            for q in range(4):
+                x = 8 * b + 8.6 + q * DMX
+                at(x, lambda b=b, q=q: mx(b, q))
+                at(x + LRL, lambda b=b, q=q: relu_store(b, q))
+            x0 = 8 * b - LRS
+            for j in range(8):
+                at(x0 + j * DRS, lambda b=b, j=j: rowsum(b, j))
+            x1 = x0 + 7 * DRS
+            at(x1 + 0.01, lambda b=b: root(b))
+            at(x1 + LRV, lambda b=b: rvec(b))
+            for hh in range(2):
+                at(x1 + LRV + 0.1 + hh * 0.01, lambda b=b, hh=hh: r_transpose(b, hh))
+                at(x1 + LRV + LRC + hh * 0.01, lambda b=b, hh=hh: r_copy(b, hh))
+            for g in range(2):
+                for t in range(4):
+                    at(
+                        x1 + LRV + LRC + 0.1 + (4 * g + t) * DRP,
+                        lambda b=b, g=g, t=t: r_plane(b, g, t),
+                    )
+        for item in sorted(plan, key=lambda it: (it[0], it[1])):
+            item[2]()

@@ -15,40 +15,41 @@ B, N, F, D = 8, 1024, 128, 256
 P = 128
 FLOPS = 2 * B * N * N * D + 2 * B * N * F * D
 
-PIN = True
-LW = 3
-XF0 = -24
-DXF = 8
-LFM = 3
-DF = 2
-LFB = 2
+LLA = 20
+LPS = 3
+LRV = 0.5
+LSQ = 3
+DRS = 1
+LW = 1.5
+LQ = 0.9
+LMX = 0.3
+LRL = 1.5
+XF0 = -14
+DXF = 6
+LFM = 2
+DF = 1.5
+LFB = 1.5
 LQF = 0.5
-DMX = 2
-LRL = 2
-LRS = 20
-DRS = 0.8
-LRV = 4
-LRC = 0.2
-DRP = 1
 VH = {}
 VHD = []
-RPW = {}
-RPWD = "GGGGGGGG"
-RG_BUFS = 3
-W_BUFS = 3
-F_BUFS = 1
-X_BUFS = 2
+PSW = {}
+PSWD = "GGGSGGGG"
+FIRST_LOADS = (("x", 0, 0), ("a", 0, 0), ("a", 0, 1), ("a", 0, 2), ("a", 0, 3), ("x", 1, 0), ("a", 1, 0), ("a", 1, 1), ("x", 2, 0), ("x", 3, 0))
+A_BUFS = 8
+T1_BUFS = 5
+W_BUFS = 4
 
 
 def tile_gcn_t_kernel(tc, inputs, adj, W_kernel, W_bias, out):
     nc = tc.nc
     with ExitStack() as ctx:
-        if PIN:
-            ctx.enter_context(tc.manual_schedule())
+        ctx.enter_context(tc.manual_schedule())
         const = ctx.enter_context(tc.tile_pool(name="const", bufs=1))
-        apool = ctx.enter_context(tc.tile_pool(name="apool", bufs=4))
-        rpool = ctx.enter_context(tc.tile_pool(name="rpool", bufs=RG_BUFS))
+        apool = ctx.enter_context(tc.tile_pool(name="apool", bufs=A_BUFS))
+        tpool = ctx.enter_context(tc.tile_pool(name="tpool", bufs=T1_BUFS))
         work = ctx.enter_context(tc.tile_pool(name="work", bufs=2))
+        qpool = ctx.enter_context(tc.tile_pool(name="qpool", bufs=3))
+        cpool = ctx.enter_context(tc.tile_pool(name="cpool", bufs=4))
         small = ctx.enter_context(tc.tile_pool(name="small", bufs=3))
         keep = ctx.enter_context(tc.tile_pool(name="keep", bufs=B))
         opool = ctx.enter_context(tc.tile_pool(name="opool", bufs=4))
@@ -66,7 +67,7 @@ def tile_gcn_t_kernel(tc, inputs, adj, W_kernel, W_bias, out):
         bias_bc = const.tile([P, D], BF16, name="bias_bc")
         nc.sync.dma_start(out=bias_bc[:], in_=W_bias.partition_broadcast(P))
         x_sb = const.tile([P, B, 8, F], BF16, name="x_sb")
-        xv = inputs.rearrange("b (q p e) f -> p b q (e f)", q=4, p=P, e=2)
+        xv = inputs.rearrange("b (j p) f -> p b j f", p=P)
         junk = const.tile([P, N], BF16, name="junk")
         junkv = const.tile([P, N // 2], F32, name="junkv") if (VH or VHD) else None
 
@@ -77,20 +78,16 @@ def tile_gcn_t_kernel(tc, inputs, adj, W_kernel, W_bias, out):
             plan.append((x, len(plan), fn))
 
         def load_x(i):
-            nc.sync.dma_start(
-                out=x_sb[:, 2 * i : 2 * i + 2].rearrange("p b (q e) f -> p b q (e f)", q=4, e=2),
-                in_=xv[:, 2 * i : 2 * i + 2],
-            )
+            nc.sync.dma_start(out=x_sb[:, 2 * i : 2 * i + 2], in_=xv[:, 2 * i : 2 * i + 2])
 
-        def load_a(b, q):
-            if q == 0:
-                a_new = apool.tile([P, 8, N], BF16, name="a_sb")
-                st[("a", b)] = a_new
-            av = adj[b].rearrange("(q p e) m -> p q e m", q=4, p=P, e=2)
-            nc.sync.dma_start(out=st[("a", b)][:, 2 * q : 2 * q + 2, :], in_=av[:, q])
+        def load_a(b, c):
+            a_sb = apool.tile([P, 2, N], BF16, name="a_sb")
+            av = adj[b].rearrange("(j p) m -> p j m", p=P)
+            nc.sync.dma_start(out=a_sb[:], in_=av[:, 2 * c : 2 * c + 2, :])
+            st[("a", b, c)] = a_sb
 
         def x_transpose(b):
-            xtp = psum.tile([P, 8, P], BF16, name="xtp", tag="x", bufs=X_BUFS)
+            xtp = psum.tile([P, 8, P], BF16, name="xtp", tag="x", bufs=1)
             for j in range(8):
                 nc.tensor.transpose(xtp[:, j, :], x_sb[:, b, j, :], ident_b[:])
             st[("xtp", b)] = xtp
@@ -102,7 +99,7 @@ def tile_gcn_t_kernel(tc, inputs, adj, W_kernel, W_bias, out):
 
         def f_matmul(b, i):
             g, h = divmod(i, 2)
-            fp = psum.tile([P, 4, P], F32, name="fp", tag="f", bufs=F_BUFS)
+            fp = psum.tile([P, 4, P], F32, name="fp", tag="f", bufs=1)
             for t in range(4):
                 nc.tensor.matmul(
                     fp[:, t, :],
@@ -139,7 +136,7 @@ def tile_gcn_t_kernel(tc, inputs, adj, W_kernel, W_bias, out):
             return VH.get(b, VHD)
 
         def rowsum(b, j):
-            a_sb = st[("a", b)]
+            a_row = st[("a", b, j // 2)][:, j % 2, :]
             if j == 0:
                 deg_new = small.tile([P, 8], F32, name="deg")
                 st[("deg", b)] = deg_new
@@ -149,19 +146,16 @@ def tile_gcn_t_kernel(tc, inputs, adj, W_kernel, W_bias, out):
             if j in vh_of(b):
                 nc.vector.scalar_tensor_tensor(
                     out=junkv[:],
-                    in0=a_sb[:, j, 0 : N // 2],
+                    in0=a_row[:, 0 : N // 2],
                     scalar=1.0,
-                    in1=a_sb[:, j, N // 2 : N],
+                    in1=a_row[:, N // 2 : N],
                     op0=ALU.mult,
                     op1=ALU.add,
                     accum_out=st[("degv", b)][:, j : j + 1],
                 )
             else:
                 nc.scalar.activation(
-                    out=junk[:],
-                    in_=a_sb[:, j, :],
-                    func=ACT.Copy,
-                    accum_out=st[("deg", b)][:, j : j + 1],
+                    out=junk[:], in_=a_row, func=ACT.Copy, accum_out=st[("deg", b)][:, j : j + 1]
                 )
 
         def runs(b):
@@ -197,128 +191,102 @@ def tile_gcn_t_kernel(tc, inputs, adj, W_kernel, W_bias, out):
                 )
             st[("r", b)] = r
 
-        def r_transpose(b, hh):
-            rnp = psum.tile([P, 4, P], F32, name="rnp", tag="x", bufs=X_BUFS)
-            r = st[("r", b)]
-            for jj in range(4):
-                j = 4 * hh + jj
-                nc.tensor.transpose(rnp[:, jj, :], r[:, j : j + 1].to_broadcast([P, P]), ident_f[:])
-            st[("rnp", b, hh)] = rnp
-
-        def r_copy(b, hh):
-            if hh == 0:
-                rn_new = work.tile([P, N], F32, name="rn")
-                st[("rn", b)] = rn_new
-            nc.scalar.copy(
-                out=st[("rn", b)][:, hh * 512 : (hh + 1) * 512],
-                in_=st[("rnp", b, hh)][:].rearrange("p a c -> p (a c)"),
-            )
-
-        def r_plane(b, g, t):
-            if t == 0:
-                rg_new = rpool.tile([P, 4, N], F32, name="rg")
-                st[("rg", b, g)] = rg_new
-            who = RPW.get(b, RPWD)[4 * g + t]
-            dst = st[("rg", b, g)][:, t, :]
-            src = st[("rn", b)][:]
-            sc = st[("r", b)][:, 4 * g + t : 4 * g + t + 1]
+        def prescale(b, j):
+            t1 = tpool.tile([P, N], F32, name="t1")
+            who = PSW.get(b, PSWD)[j]
+            src = st[("a", b, j // 2)][:, j % 2, :]
+            sc = st[("r", b)][:, j : j + 1]
             if who == "G":
                 nc.gpsimd.tensor_scalar(
-                    out=dst, in0=src, scalar1=sc, scalar2=0.0, op0=ALU.mult, op1=ALU.add
+                    out=t1[:], in0=src, scalar1=sc, scalar2=0.0, op0=ALU.mult, op1=ALU.add
                 )
             elif who == "V":
-                nc.vector.tensor_scalar_mul(out=dst, in0=src, scalar1=sc)
+                nc.vector.tensor_scalar_mul(out=t1[:], in0=src, scalar1=sc)
             else:
-                nc.scalar.activation(out=dst, in_=src, func=ACT.Copy, scale=sc)
+                nc.scalar.activation(out=t1[:], in_=src, func=ACT.Copy, scale=sc)
+            st[("t1", b, j)] = t1
 
-        def a_transpose(b, s):
-            g, nb = divmod(s, 4)
-            a_sb = st[("a", b)]
-            tp = psum.tile([P, 512], F32, name="tp", tag="w", bufs=W_BUFS)
-            for u in range(2):
-                for jj in range(2):
-                    j = 2 * nb + jj
-                    c0 = 256 * g + 128 * u
-                    nc.tensor.transpose(
-                        tp[:, u * 256 + jj * P : u * 256 + (jj + 1) * P],
-                        a_sb[:, j, :].bitcast(F32)[:, c0 : c0 + P],
-                        ident_f[:],
-                    )
-            st[("tp", b, s)] = tp
+        def a_transpose(b, j, g):
+            tp = psum.tile([P, 4, P], F32, name="tp", tag="w", bufs=W_BUFS)
+            t1 = st[("t1", b, j)]
+            for t in range(4):
+                c0 = 512 * g + P * t
+                nc.tensor.transpose(tp[:, t, :], t1[:, c0 : c0 + P], ident_f[:])
+            st[("tp", b, j, g)] = tp
 
-        def a_scale(b, s):
-            g, nb = divmod(s, 4)
-            if nb == 0:
-                gq_new = work.tile([P, N, 4], BF16, name="gq", align_bytes=64)
-                st[("gq", b, g)] = gq_new
+        def a_scale(b, j, g):
+            if g == 0:
+                gq_new = qpool.tile([P, 2, P, 4], BF16, name="gq", align_bytes=64)
+                st[("gq", b, j)] = gq_new
             nc.vector.tensor_tensor(
-                out=st[("gq", b, g)][:, nb * 256 : (nb + 1) * 256, :].rearrange(
-                    "p n (u e) -> p n u e", u=2, e=2
-                ),
-                in0=st[("tp", b, s)][:]
-                .bitcast(BF16)
-                .rearrange("p (u n e) -> p n u e", u=2, n=256, e=2),
-                in1=st[("rg", b, g)][:, :, nb * 256 : (nb + 1) * 256].rearrange(
-                    "p (u e) n -> p n u e", u=2, e=2
-                ),
+                out=st[("gq", b, j)][:, g, :, :],
+                in0=st[("tp", b, j, g)][:].rearrange("p t n -> p n t"),
+                in1=st[("r", b)][:, 4 * g : 4 * g + 4].unsqueeze(1).to_broadcast([P, P, 4]),
                 op=ALU.mult,
             )
 
-        def a_quant(b, g):
-            if g == 0:
-                ac_new = work.tile([P, 2 * N], U32, name="ac", align_bytes=64)
-                asc_new = work.tile([P, 2 * N], U8, name="asc", align_bytes=64)
-                st[("ac", b)] = (ac_new, asc_new)
-            ac, asc = st[("ac", b)]
+        def a_quant(b, j):
+            ac = cpool.tile([P, 2 * P], U32, name="ac", align_bytes=64)
+            asc = cpool.tile([P, 2 * P], U8, name="asc", align_bytes=64)
             nc.vector.quantize_mx(
-                out=ac[:, g * N : (g + 1) * N].bitcast(FP8X4),
-                scales=asc[:, g * N : (g + 1) * N],
-                in_=st[("gq", b, g)][:].rearrange("p n t -> p (n t)"),
+                out=ac[:].bitcast(FP8X4),
+                scales=asc[:],
+                in_=st[("gq", b, j)][:].rearrange("p g n t -> p (g n t)"),
             )
+            st[("ac", b, j)] = (ac, asc)
 
-        def mx(b, q):
-            ac, asc = st[("ac", b)]
+        def mx(b, j):
+            ac, asc = st[("ac", b, j)]
             fc, fs = st[("fc", b)]
-            op = psum.tile([P, 2, D], F32, name="op", tag="o", bufs=2)
-            for e in range(2):
-                j = 2 * q + e
-                for g in range(2):
-                    c0 = g * N + j * P
-                    nc.tensor.matmul_mx(
-                        out=op[:, e, :],
-                        lhsT=ac[:, c0 : c0 + P].bitcast(FP8X4),
-                        lhsT_scale=asc[:, c0 : c0 + P],
-                        rhs=fc[:, g * D : (g + 1) * D].bitcast(FP8X4),
-                        rhs_scale=fs[:, g * D : (g + 1) * D],
-                        start=(g == 0),
-                        stop=(g == 1),
-                    )
-            st[("op", b, q)] = op
+            if j % 2 == 0:
+                op_new = psum.tile([P, 2, D], F32, name="op", tag="o", bufs=2)
+                st[("op", b, j // 2)] = op_new
+            op = st[("op", b, j // 2)]
+            for g in range(2):
+                nc.tensor.matmul_mx(
+                    out=op[:, j % 2, :],
+                    lhsT=ac[:, g * P : (g + 1) * P].bitcast(FP8X4),
+                    lhsT_scale=asc[:, g * P : (g + 1) * P],
+                    rhs=fc[:, g * D : (g + 1) * D].bitcast(FP8X4),
+                    rhs_scale=fs[:, g * D : (g + 1) * D],
+                    start=(g == 0),
+                    stop=(g == 1),
+                )
 
-        def relu_store(b, q):
-            ov = out[b].rearrange("(q p e) d -> p q e d", q=4, p=P, e=2)
+        def relu_store(b, c):
+            ov = out[b].rearrange("(j p) d -> p j d", p=P)
             o_sb = opool.tile([P, 2, D], F32, name="o_sb")
-            nc.scalar.activation(out=o_sb[:], in_=st[("op", b, q)][:], func=ACT.Relu)
-            nc.scalar.dma_start(out=ov[:, q], in_=o_sb[:])
+            nc.scalar.activation(out=o_sb[:], in_=st[("op", b, c)][:], func=ACT.Relu)
+            nc.scalar.dma_start(out=ov[:, 2 * c : 2 * c + 2, :], in_=o_sb[:])
 
         lx = -1000.0
-        for kind, i in (("x", 0), ("a", 0), ("x", 1), ("a", 1), ("x", 2), ("x", 3), ("a", 2), ("a", 3)):
+        first = set()
+        for kind, i, c in FIRST_LOADS:
+            lx += 0.01
             if kind == "x":
-                lx += 0.01
                 at(lx, lambda i=i: load_x(i))
             else:
-                for q in range(4):
-                    lx += 0.01
-                    at(lx, lambda i=i, q=q: load_a(i, q))
-        for b in range(4, B):
-            for q in range(4):
-                at(8 * (b - 4) + 7 - LW + 0.3 + q * 0.01, lambda b=b, q=q: load_a(b, q))
+                first.add((i, c))
+                at(lx, lambda i=i, c=c: load_a(i, c))
         for b in range(B):
-            for s in range(8):
-                at(8 * b + s - LW - 0.5, lambda b=b, s=s: a_transpose(b, s))
-                at(8 * b + s, lambda b=b, s=s: a_scale(b, s))
-            at(8 * b + 4.5, lambda b=b: a_quant(b, 0))
-            at(8 * b + 8.5, lambda b=b: a_quant(b, 1))
+            for c in range(4):
+                if (b, c) not in first:
+                    at(8 * b + 2 * c - LLA, lambda b=b, c=c: load_a(b, c))
+            xr = 8 * b - LPS - LRV - LSQ
+            for j in range(8):
+                at(xr - (7 - j) * DRS, lambda b=b, j=j: rowsum(b, j))
+            at(xr + 0.01, lambda b=b: root(b))
+            at(xr + LSQ, lambda b=b: rvec(b))
+            for j in range(8):
+                i = 8 * b + j
+                at(i - LPS, lambda b=b, j=j: prescale(b, j))
+                for g in range(2):
+                    at(i - LW + 0.4 * g, lambda b=b, j=j, g=g: a_transpose(b, j, g))
+                    at(i + 0.4 * g, lambda b=b, j=j, g=g: a_scale(b, j, g))
+                at(i + LQ, lambda b=b, j=j: a_quant(b, j))
+                at(i + LQ + LMX, lambda b=b, j=j: mx(b, j))
+                if j % 2 == 1:
+                    at(i + LQ + LMX + LRL, lambda b=b, j=j: relu_store(b, j // 2))
             x0 = XF0 + b * DXF
             at(x0, lambda b=b: x_transpose(b))
             at(x0 + 0.05, lambda b=b: x_copy(b))
@@ -326,24 +294,5 @@ def tile_gcn_t_kernel(tc, inputs, adj, W_kernel, W_bias, out):
                 at(x0 + LFM + i * DF, lambda b=b, i=i: f_matmul(b, i))
                 at(x0 + LFM + i * DF + LFB, lambda b=b, i=i: f_bias(b, i))
             at(x0 + LFM + 3 * DF + LFB + LQF, lambda b=b: f_quant(b))
-            for q in range(4):
-                x = 8 * b + 8.6 + q * DMX
-                at(x, lambda b=b, q=q: mx(b, q))
-                at(x + LRL, lambda b=b, q=q: relu_store(b, q))
-            x0 = 8 * b - LRS
-            for j in range(8):
-                at(x0 + j * DRS, lambda b=b, j=j: rowsum(b, j))
-            x1 = x0 + 7 * DRS
-            at(x1 + 0.01, lambda b=b: root(b))
-            at(x1 + LRV, lambda b=b: rvec(b))
-            for hh in range(2):
-                at(x1 + LRV + 0.1 + hh * 0.01, lambda b=b, hh=hh: r_transpose(b, hh))
-                at(x1 + LRV + LRC + hh * 0.01, lambda b=b, hh=hh: r_copy(b, hh))
-            for g in range(2):
-                for t in range(4):
-                    at(
-                        x1 + LRV + LRC + 0.1 + (4 * g + t) * DRP,
-                        lambda b=b, g=g, t=t: r_plane(b, g, t),
-                    )
         for item in sorted(plan, key=lambda it: (it[0], it[1])):
             item[2]()

@@ -15,21 +15,21 @@ B, N, F, D = 8, 1024, 128, 256
 P = 128
 FLOPS = 2 * B * N * N * D + 2 * B * N * F * D
 
-LLA = 20
-LPS = 3
+LLA = 14
+LPS = 3.5
 LRV = 0.5
-LSQ = 3
-DRS = 1
+LSQ = 2
+DRS = 1.1
 LW = 1.5
 LQ = 0.9
 LMX = 0.3
-LRL = 1.5
+LRL = 0.5
 XF0 = -14
-DXF = 6
+DXF = 8
 LFM = 2
-DF = 1.5
+DF = 2
 LFB = 1.5
-LQF = 0.5
+LQF = 1
 VH = {}
 VHD = []
 PSW = {}
@@ -123,12 +123,17 @@ def tile_gcn_t_kernel(tc, inputs, adj, W_kernel, W_bias, out):
             )
 
         def f_quant(b):
-            fc = keep.tile([P, 2 * D], U32, name="fc", align_bytes=64)
-            fs = keep.tile([P, 2 * D], U8, name="fs", align_bytes=64)
+            fc = keep.tile([P, 3 * D], U32, name="fc", align_bytes=64)
+            fs = keep.tile([P, 3 * D], U8, name="fs", align_bytes=64)
             nc.vector.quantize_mx(
-                out=fc[:].bitcast(FP8X4),
-                scales=fs[:],
+                out=fc[:, 0 : 2 * D].bitcast(FP8X4),
+                scales=fs[:, 0 : 2 * D],
                 in_=st[("fg", b)][:].rearrange("p g d t -> p (g d t)"),
+            )
+            nc.vector.quantize_mx(
+                out=fc[:, 2 * D : 3 * D].bitcast(FP8X4),
+                scales=fs[:, 2 * D : 3 * D],
+                in_=st[("fg", b)][:, 0].rearrange("p d t -> p (d t)"),
             )
             st[("fc", b)] = (fc, fs)
 
@@ -238,26 +243,28 @@ def tile_gcn_t_kernel(tc, inputs, adj, W_kernel, W_bias, out):
         def mx(b, j):
             ac, asc = st[("ac", b, j)]
             fc, fs = st[("fc", b)]
-            if j % 2 == 0:
-                op_new = psum.tile([P, 2, D], F32, name="op", tag="o", bufs=2)
-                st[("op", b, j // 2)] = op_new
-            op = st[("op", b, j // 2)]
+            op = psum.tile([P, 2 * D], F32, name="op", tag="o", bufs=2)
+            st[("op", b, j)] = op
             for g in range(2):
                 nc.tensor.matmul_mx(
-                    out=op[:, j % 2, :],
+                    out=op[:],
                     lhsT=ac[:, g * P : (g + 1) * P].bitcast(FP8X4),
                     lhsT_scale=asc[:, g * P : (g + 1) * P],
-                    rhs=fc[:, g * D : (g + 1) * D].bitcast(FP8X4),
-                    rhs_scale=fs[:, g * D : (g + 1) * D],
+                    rhs=fc[:, g * D : (g + 2) * D].bitcast(FP8X4),
+                    rhs_scale=fs[:, g * D : (g + 2) * D],
                     start=(g == 0),
                     stop=(g == 1),
                 )
 
-        def relu_store(b, c):
-            ov = out[b].rearrange("(j p) d -> p j d", p=P)
-            o_sb = opool.tile([P, 2, D], F32, name="o_sb")
-            nc.scalar.activation(out=o_sb[:], in_=st[("op", b, c)][:], func=ACT.Relu)
-            nc.scalar.dma_start(out=ov[:, 2 * c : 2 * c + 2, :], in_=o_sb[:])
+        def relu_store(b, j):
+            if j % 2 == 0:
+                o_new = opool.tile([P, 2, D], F32, name="o_sb")
+                st[("o", b, j // 2)] = o_new
+            o_sb = st[("o", b, j // 2)]
+            nc.scalar.activation(out=o_sb[:, j % 2, :], in_=st[("op", b, j)][:, 0:D], func=ACT.Relu)
+            if j % 2 == 1:
+                ov = out[b].rearrange("(j p) d -> p j d", p=P)
+                nc.scalar.dma_start(out=ov[:, j - 1 : j + 1, :], in_=o_sb[:])
 
         lx = -1000.0
         first = set()
@@ -285,8 +292,7 @@ def tile_gcn_t_kernel(tc, inputs, adj, W_kernel, W_bias, out):
                     at(i + 0.4 * g, lambda b=b, j=j, g=g: a_scale(b, j, g))
                 at(i + LQ, lambda b=b, j=j: a_quant(b, j))
                 at(i + LQ + LMX, lambda b=b, j=j: mx(b, j))
-                if j % 2 == 1:
-                    at(i + LQ + LMX + LRL, lambda b=b, j=j: relu_store(b, j // 2))
+                at(i + LQ + LMX + LRL, lambda b=b, j=j: relu_store(b, j))
             x0 = XF0 + b * DXF
             at(x0, lambda b=b: x_transpose(b))
             at(x0 + 0.05, lambda b=b: x_copy(b))

@@ -16,24 +16,24 @@ P = 128
 FLOPS = 2 * B * N * N * D + 2 * B * N * F * D
 
 LLA = 14
-LPS = 3.5
+LPS = 2.5
 LRV = 0.5
-LSQ = 2
-DRS = 1.1
-LW = 1.5
-LQ = 0.9
-LMX = 0.3
+LSQ = 1
+DRS = 1
+LW = 1
+LQ = 1.2
+LMX = 1.5
 LRL = 0.5
 XF0 = -14
 DXF = 8
-LFM = 2
-DF = 2
-LFB = 1.5
-LQF = 1
+LFM = 1
+DF = 1.5
+LFB = 1
+LQF = 0.5
 VH = {}
 VHD = []
 PSW = {}
-PSWD = "GGGSGGGG"
+PSWD = "SGVGSGVG"
 FIRST_LOADS = (("x", 0, 0), ("a", 0, 0), ("a", 0, 1), ("a", 0, 2), ("a", 0, 3), ("x", 1, 0), ("a", 1, 0), ("a", 1, 1), ("x", 2, 0), ("x", 3, 0))
 A_BUFS = 8
 T1_BUFS = 5

@@ -16,24 +16,24 @@ P = 128
 FLOPS = 2 * B * N * N * D + 2 * B * N * F * D
 
 LLA = 14
-LPS = 2.5
+LPS = 3.5
 LRV = 0.5
-LSQ = 1
-DRS = 1
-LW = 1
-LQ = 1.2
-LMX = 1.5
+LSQ = 2
+DRS = 1.1
+LW = 1.5
+LQ = 0.9
+LMX = 0.3
 LRL = 0.5
 XF0 = -14
 DXF = 8
-LFM = 1
-DF = 1.5
-LFB = 1
-LQF = 0.5
+LFM = 2
+DF = 2
+LFB = 1.5
+LQF = 1
 VH = {}
 VHD = []
 PSW = {}
-PSWD = "SGVGSGVG"
+PSWD = "GGGSGGGG"
 FIRST_LOADS = (("x", 0, 0), ("a", 0, 0), ("a", 0, 1), ("a", 0, 2), ("a", 0, 3), ("x", 1, 0), ("a", 1, 0), ("a", 1, 1), ("x", 2, 0), ("x", 3, 0))
 A_BUFS = 8
 T1_BUFS = 5
@@ -116,9 +116,12 @@ def tile_gcn_t_kernel(tc, inputs, adj, W_kernel, W_bias, out):
                 fg_new = work.tile([P, 2, D, 4], BF16, name="fg", align_bytes=64)
                 st[("fg", b)] = fg_new
             nc.vector.tensor_tensor(
-                out=st[("fg", b)][:, g, h * P : (h + 1) * P, :],
-                in0=st[("fp", b, i)][:].rearrange("p t d -> p d t"),
-                in1=bias_bc[:, h * P : (h + 1) * P].unsqueeze(2).to_broadcast([P, P, 4]),
+                out=st[("fg", b)][:, g, h * P : (h + 1) * P, :].rearrange("p (c i) t -> p c t i", i=4),
+                in0=st[("fp", b, i)][:].rearrange("p t (c i) -> p c t i", i=4),
+                in1=bias_bc[:, h * P : (h + 1) * P]
+                .rearrange("p (c i) -> p c i", i=4)
+                .unsqueeze(2)
+                .to_broadcast([P, P // 4, 4, 4]),
                 op=ALU.add,
             )
 
@@ -224,9 +227,12 @@ def tile_gcn_t_kernel(tc, inputs, adj, W_kernel, W_bias, out):
                 gq_new = qpool.tile([P, 2, P, 4], BF16, name="gq", align_bytes=64)
                 st[("gq", b, j)] = gq_new
             nc.vector.tensor_tensor(
-                out=st[("gq", b, j)][:, g, :, :],
-                in0=st[("tp", b, j, g)][:].rearrange("p t n -> p n t"),
-                in1=st[("r", b)][:, 4 * g : 4 * g + 4].unsqueeze(1).to_broadcast([P, P, 4]),
+                out=st[("gq", b, j)][:, g, :, :].rearrange("p (c i) t -> p c t i", i=4),
+                in0=st[("tp", b, j, g)][:].rearrange("p t (c i) -> p c t i", i=4),
+                in1=st[("r", b)][:, 4 * g : 4 * g + 4]
+                .unsqueeze(1)
+                .unsqueeze(3)
+                .to_broadcast([P, P // 4, 4, 4]),
                 op=ALU.mult,
             )
 

@@ -15,25 +15,25 @@ B, N, F, D = 8, 1024, 128, 256
 P = 128
 FLOPS = 2 * B * N * N * D + 2 * B * N * F * D
 
-LLA = 14
+LLA = 20
 LPS = 3.5
 LRV = 0.5
 LSQ = 2
 DRS = 1.1
 LW = 1.5
 LQ = 0.9
-LMX = 0.3
+LMX = 1.5
 LRL = 0.5
 XF0 = -14
-DXF = 8
+DXF = 7
 LFM = 2
 DF = 2
-LFB = 1.5
-LQF = 1
+LFB = 1
+LQF = 0.5
 VH = {}
 VHD = []
 PSW = {}
-PSWD = "GGGSGGGG"
+PSWD = "GGSGGSGS"
 FIRST_LOADS = (("x", 0, 0), ("a", 0, 0), ("a", 0, 1), ("a", 0, 2), ("a", 0, 3), ("x", 1, 0), ("a", 1, 0), ("a", 1, 1), ("x", 2, 0), ("x", 3, 0))
 A_BUFS = 8
 T1_BUFS = 5
@@ -116,12 +116,9 @@ def tile_gcn_t_kernel(tc, inputs, adj, W_kernel, W_bias, out):
                 fg_new = work.tile([P, 2, D, 4], BF16, name="fg", align_bytes=64)
                 st[("fg", b)] = fg_new
             nc.vector.tensor_tensor(
-                out=st[("fg", b)][:, g, h * P : (h + 1) * P, :].rearrange("p (c i) t -> p c t i", i=4),
-                in0=st[("fp", b, i)][:].rearrange("p t (c i) -> p c t i", i=4),
-                in1=bias_bc[:, h * P : (h + 1) * P]
-                .rearrange("p (c i) -> p c i", i=4)
-                .unsqueeze(2)
-                .to_broadcast([P, P // 4, 4, 4]),
+                out=st[("fg", b)][:, g, h * P : (h + 1) * P, :],
+                in0=st[("fp", b, i)][:].rearrange("p t d -> p d t"),
+                in1=bias_bc[:, h * P : (h + 1) * P].unsqueeze(2).to_broadcast([P, P, 4]),
                 op=ALU.add,
             )
 
@@ -227,12 +224,9 @@ def tile_gcn_t_kernel(tc, inputs, adj, W_kernel, W_bias, out):
                 gq_new = qpool.tile([P, 2, P, 4], BF16, name="gq", align_bytes=64)
                 st[("gq", b, j)] = gq_new
             nc.vector.tensor_tensor(
-                out=st[("gq", b, j)][:, g, :, :].rearrange("p (c i) t -> p c t i", i=4),
-                in0=st[("tp", b, j, g)][:].rearrange("p t (c i) -> p c t i", i=4),
-                in1=st[("r", b)][:, 4 * g : 4 * g + 4]
-                .unsqueeze(1)
-                .unsqueeze(3)
-                .to_broadcast([P, P // 4, 4, 4]),
+                out=st[("gq", b, j)][:, g, :, :],
+                in0=st[("tp", b, j, g)][:].rearrange("p t n -> p n t"),
+                in1=st[("r", b)][:, 4 * g : 4 * g + 4].unsqueeze(1).to_broadcast([P, P, 4]),
                 op=ALU.mult,
             )
 

@@ -15,25 +15,25 @@ B, N, F, D = 8, 1024, 128, 256
 P = 128
 FLOPS = 2 * B * N * N * D + 2 * B * N * F * D
 
-LLA = 20
-LPS = 3.5
-LRV = 0.5
-LSQ = 2
+LLA = 18
+LPS = 2.5
+LRV = 1
+LSQ = 1
 DRS = 1.1
 LW = 1.5
-LQ = 0.9
-LMX = 1.5
-LRL = 0.5
-XF0 = -14
-DXF = 7
-LFM = 2
+LQ = 1.3
+LMX = 0.3
+LRL = 1
+XF0 = -12
+DXF = 8
+LFM = 1
 DF = 2
-LFB = 1
-LQF = 0.5
+LFB = 1.5
+LQF = 1
 VH = {}
 VHD = []
 PSW = {}
-PSWD = "GGSGGSGS"
+PSWD = "GGGGGGGG"
 FIRST_LOADS = (("x", 0, 0), ("a", 0, 0), ("a", 0, 1), ("a", 0, 2), ("a", 0, 3), ("x", 1, 0), ("a", 1, 0), ("a", 1, 1), ("x", 2, 0), ("x", 3, 0))
 A_BUFS = 8
 T1_BUFS = 5
@@ -245,6 +245,16 @@ def tile_gcn_t_kernel(tc, inputs, adj, W_kernel, W_bias, out):
             fc, fs = st[("fc", b)]
             op = psum.tile([P, 2 * D], F32, name="op", tag="o", bufs=2)
             st[("op", b, j)] = op
+            for k in range(2):
+                nc.tensor.matmul_mx(
+                    out=op[:, D : 2 * D],
+                    lhsT=fc[:, 0:P].bitcast(FP8X4),
+                    lhsT_scale=fs[:, 0:P],
+                    rhs=fc[:, D : 2 * D].bitcast(FP8X4),
+                    rhs_scale=fs[:, D : 2 * D],
+                    start=True,
+                    stop=True,
+                )
             for g in range(2):
                 nc.tensor.matmul_mx(
                     out=op[:],

@@ -15,18 +15,18 @@ B, N, F, D = 8, 1024, 128, 256
 P = 128
 FLOPS = 2 * B * N * N * D + 2 * B * N * F * D
 
-LLA = 18
-LPS = 2.5
-LRV = 1
-LSQ = 1
-DRS = 1.1
-LW = 1.5
+LLA = 20
+LPS = 4.5
+LRV = 1.5
+LSQ = 1.5
+DRS = 1
+LW = 2.8
 LQ = 1.3
-LMX = 0.3
-LRL = 1
+LMX = 1
+LRL = 1.5
 XF0 = -12
 DXF = 8
-LFM = 1
+LFM = 2
 DF = 2
 LFB = 1.5
 LQF = 1
@@ -34,10 +34,10 @@ VH = {}
 VHD = []
 PSW = {}
 PSWD = "GGGGGGGG"
-FIRST_LOADS = (("x", 0, 0), ("a", 0, 0), ("a", 0, 1), ("a", 0, 2), ("a", 0, 3), ("x", 1, 0), ("a", 1, 0), ("a", 1, 1), ("x", 2, 0), ("x", 3, 0))
-A_BUFS = 8
-T1_BUFS = 5
-W_BUFS = 4
+FIRST_LOADS = (("a", 0, 0), ("a", 0, 1), ("x", 0, 0), ("a", 0, 2), ("a", 0, 3), ("x", 1, 0), ("a", 1, 0), ("a", 1, 1), ("x", 2, 0), ("x", 3, 0))
+A_BUFS = 12
+T1_BUFS = 8
+W_BUFS = 6
 
 
 def tile_gcn_t_kernel(tc, inputs, adj, W_kernel, W_bias, out):
@@ -87,7 +87,7 @@ def tile_gcn_t_kernel(tc, inputs, adj, W_kernel, W_bias, out):
             st[("a", b, c)] = a_sb
 
         def x_transpose(b):
-            xtp = psum.tile([P, 8, P], BF16, name="xtp", tag="x", bufs=1)
+            xtp = psum.tile([P, 8, P], BF16, name="xtp", tag="w", bufs=W_BUFS)
             for j in range(8):
                 nc.tensor.transpose(xtp[:, j, :], x_sb[:, b, j, :], ident_b[:])
             st[("xtp", b)] = xtp
@@ -99,7 +99,7 @@ def tile_gcn_t_kernel(tc, inputs, adj, W_kernel, W_bias, out):
 
         def f_matmul(b, i):
             g, h = divmod(i, 2)
-            fp = psum.tile([P, 4, P], F32, name="fp", tag="f", bufs=1)
+            fp = psum.tile([P, 4, P], F32, name="fp", tag="w", bufs=W_BUFS)
             for t in range(4):
                 nc.tensor.matmul(
                     fp[:, t, :],
@@ -123,17 +123,12 @@ def tile_gcn_t_kernel(tc, inputs, adj, W_kernel, W_bias, out):
             )
 
         def f_quant(b):
-            fc = keep.tile([P, 3 * D], U32, name="fc", align_bytes=64)
-            fs = keep.tile([P, 3 * D], U8, name="fs", align_bytes=64)
+            fc = keep.tile([P, 2 * D], U32, name="fc", align_bytes=64)
+            fs = keep.tile([P, 2 * D], U8, name="fs", align_bytes=64)
             nc.vector.quantize_mx(
-                out=fc[:, 0 : 2 * D].bitcast(FP8X4),
-                scales=fs[:, 0 : 2 * D],
+                out=fc[:].bitcast(FP8X4),
+                scales=fs[:],
                 in_=st[("fg", b)][:].rearrange("p g d t -> p (g d t)"),
-            )
-            nc.vector.quantize_mx(
-                out=fc[:, 2 * D : 3 * D].bitcast(FP8X4),
-                scales=fs[:, 2 * D : 3 * D],
-                in_=st[("fg", b)][:, 0].rearrange("p d t -> p (d t)"),
             )
             st[("fc", b)] = (fc, fs)
 
@@ -243,11 +238,13 @@ def tile_gcn_t_kernel(tc, inputs, adj, W_kernel, W_bias, out):
         def mx(b, j):
             ac, asc = st[("ac", b, j)]
             fc, fs = st[("fc", b)]
-            op = psum.tile([P, 2 * D], F32, name="op", tag="o", bufs=2)
-            st[("op", b, j)] = op
-            for k in range(2):
+            if j % 2 == 0:
+                op_new = psum.tile([P, 2, D], F32, name="op", tag="o", bufs=2)
+                st[("op", b, j // 2)] = op_new
+            op = st[("op", b, j // 2)]
+            for k in range(3):
                 nc.tensor.matmul_mx(
-                    out=op[:, D : 2 * D],
+                    out=op[:, j % 2, :],
                     lhsT=fc[:, 0:P].bitcast(FP8X4),
                     lhsT_scale=fs[:, 0:P],
                     rhs=fc[:, D : 2 * D].bitcast(FP8X4),
@@ -257,24 +254,20 @@ def tile_gcn_t_kernel(tc, inputs, adj, W_kernel, W_bias, out):
                 )
             for g in range(2):
                 nc.tensor.matmul_mx(
-                    out=op[:],
+                    out=op[:, j % 2, :],
                     lhsT=ac[:, g * P : (g + 1) * P].bitcast(FP8X4),
                     lhsT_scale=asc[:, g * P : (g + 1) * P],
-                    rhs=fc[:, g * D : (g + 2) * D].bitcast(FP8X4),
-                    rhs_scale=fs[:, g * D : (g + 2) * D],
+                    rhs=fc[:, g * D : (g + 1) * D].bitcast(FP8X4),
+                    rhs_scale=fs[:, g * D : (g + 1) * D],
                     start=(g == 0),
                     stop=(g == 1),
                 )
 
-        def relu_store(b, j):
-            if j % 2 == 0:
-                o_new = opool.tile([P, 2, D], F32, name="o_sb")
-                st[("o", b, j // 2)] = o_new
-            o_sb = st[("o", b, j // 2)]
-            nc.scalar.activation(out=o_sb[:, j % 2, :], in_=st[("op", b, j)][:, 0:D], func=ACT.Relu)
-            if j % 2 == 1:
-                ov = out[b].rearrange("(j p) d -> p j d", p=P)
-                nc.scalar.dma_start(out=ov[:, j - 1 : j + 1, :], in_=o_sb[:])
+        def relu_store(b, c):
+            ov = out[b].rearrange("(j p) d -> p j d", p=P)
+            o_sb = opool.tile([P, 2, D], F32, name="o_sb")
+            nc.scalar.activation(out=o_sb[:], in_=st[("op", b, c)][:], func=ACT.Relu)
+            nc.scalar.dma_start(out=ov[:, 2 * c : 2 * c + 2, :], in_=o_sb[:])
 
         lx = -1000.0
         first = set()
@@ -302,10 +295,11 @@ def tile_gcn_t_kernel(tc, inputs, adj, W_kernel, W_bias, out):
                     at(i + 0.4 * g, lambda b=b, j=j, g=g: a_scale(b, j, g))
                 at(i + LQ, lambda b=b, j=j: a_quant(b, j))
                 at(i + LQ + LMX, lambda b=b, j=j: mx(b, j))
-                at(i + LQ + LMX + LRL, lambda b=b, j=j: relu_store(b, j))
+                if j % 2 == 1:
+                    at(i + LQ + LMX + LRL, lambda b=b, j=j: relu_store(b, j // 2))
             x0 = XF0 + b * DXF
             at(x0, lambda b=b: x_transpose(b))
-            at(x0 + 0.05, lambda b=b: x_copy(b))
+            at(x0 + 1.0, lambda b=b: x_copy(b))
             for i in range(4):
                 at(x0 + LFM + i * DF, lambda b=b, i=i: f_matmul(b, i))
                 at(x0 + LFM + i * DF + LFB, lambda b=b, i=i: f_bias(b, i))

from contextlib import ExitStack

import concourse.mybir as mybir
from concourse.masks import make_identity

F32 = mybir.dt.float32
BF16 = mybir.dt.bfloat16
U32 = mybir.dt.uint32
U8 = mybir.dt.uint8
FP8X4 = mybir.dt.float8_e4m3fn_x4
ALU = mybir.AluOpType
ACT = mybir.ActivationFunctionType

B, N, F, D = 8, 1024, 128, 256
P = 128
FLOPS = 2 * B * N * N * D + 2 * B * N * F * D

LLA = 20
LPS = 4.5
LRV = 1.5
LSQ = 1.5
DRS = 1
LW = 2.8
LQ = 1.3
LMX = 1
LRL = 1.5
XF0 = -12
DXF = 8
LFM = 2
DF = 2
LFB = 1.5
LQF = 1
VH = {}
VHD = []
PSW = {}
PSWD = "GGGGGGGG"
FIRST_LOADS = (("a", 0, 0), ("a", 0, 1), ("x", 0, 0), ("a", 0, 2), ("a", 0, 3), ("x", 1, 0), ("a", 1, 0), ("a", 1, 1), ("x", 2, 0), ("x", 3, 0))
A_BUFS = 12
T1_BUFS = 8
W_BUFS = 6


def tile_gcn_t_kernel(tc, inputs, adj, W_kernel, W_bias, out):
    nc = tc.nc
    with ExitStack() as ctx:
        ctx.enter_context(tc.manual_schedule())
        const = ctx.enter_context(tc.tile_pool(name="const", bufs=1))
        apool = ctx.enter_context(tc.tile_pool(name="apool", bufs=A_BUFS))
        tpool = ctx.enter_context(tc.tile_pool(name="tpool", bufs=T1_BUFS))
        work = ctx.enter_context(tc.tile_pool(name="work", bufs=2))
        qpool = ctx.enter_context(tc.tile_pool(name="qpool", bufs=3))
        cpool = ctx.enter_context(tc.tile_pool(name="cpool", bufs=4))
        small = ctx.enter_context(tc.tile_pool(name="small", bufs=3))
        keep = ctx.enter_context(tc.tile_pool(name="keep", bufs=B))
        opool = ctx.enter_context(tc.tile_pool(name="opool", bufs=4))
        psum = ctx.enter_context(tc.psum_pool(name="psum", bufs=1))

        warm = const.tile([P, 1], F32, name="warm")
        nc.vector.memset(warm[:], 1.0)
        nc.scalar.activation(out=warm[:], in_=warm[:], func=ACT.Sqrt)
        ident_b = const.tile([P, P], BF16, name="ident_b")
        make_identity(nc, ident_b[:])
        ident_f = const.tile([P, P], F32, name="ident_f")
        make_identity(nc, ident_f[:])
        w_sb = const.tile([P, D], BF16, name="w_sb")
        nc.sync.dma_start(out=w_sb[:], in_=W_kernel)
        bias_bc = const.tile([P, D], BF16, name="bias_bc")
        nc.sync.dma_start(out=bias_bc[:], in_=W_bias.partition_broadcast(P))
        x_sb = const.tile([P, B, 8, F], BF16, name="x_sb")
        xv = inputs.rearrange("b (j p) f -> p b j f", p=P)
        junk = const.tile([P, N], BF16, name="junk")
        junkv = const.tile([P, N // 2], F32, name="junkv") if (VH or VHD) else None

        st = {}
        plan = []

        def at(x, fn):
            plan.append((x, len(plan), fn))

        def load_x(i):
            nc.sync.dma_start(out=x_sb[:, 2 * i : 2 * i + 2], in_=xv[:, 2 * i : 2 * i + 2])

        def load_a(b, c):
            a_sb = apool.tile([P, 2, N], BF16, name="a_sb")
            av = adj[b].rearrange("(j p) m -> p j m", p=P)
            nc.sync.dma_start(out=a_sb[:], in_=av[:, 2 * c : 2 * c + 2, :])
            st[("a", b, c)] = a_sb

        def x_transpose(b):
            xtp = psum.tile([P, 8, P], BF16, name="xtp", tag="w", bufs=W_BUFS)
            for j in range(8):
                nc.tensor.transpose(xtp[:, j, :], x_sb[:, b, j, :], ident_b[:])
            st[("xtp", b)] = xtp

        def x_copy(b):
            xt = work.tile([P, 8, P], BF16, name="xt")
            nc.scalar.copy(out=xt[:], in_=st[("xtp", b)][:])
            st[("xt", b)] = xt

        def f_matmul(b, i):
            g, h = divmod(i, 2)
            fp = psum.tile([P, 4, P], F32, name="fp", tag="w", bufs=W_BUFS)
            for t in range(4):
                nc.tensor.matmul(
                    fp[:, t, :],
                    lhsT=st[("xt", b)][:, 4 * g + t, :],
                    rhs=w_sb[:, h * P : (h + 1) * P],
                    start=True,
                    stop=True,
                )
            st[("fp", b, i)] = fp

        def f_bias(b, i):
            g, h = divmod(i, 2)
            if i == 0:
                fg_new = work.tile([P, 2, D, 4], BF16, name="fg", align_bytes=64)
                st[("fg", b)] = fg_new
            nc.vector.tensor_tensor(
                out=st[("fg", b)][:, g, h * P : (h + 1) * P, :],
                in0=st[("fp", b, i)][:].rearrange("p t d -> p d t"),
                in1=bias_bc[:, h * P : (h + 1) * P].unsqueeze(2).to_broadcast([P, P, 4]),
                op=ALU.add,
            )

        def f_quant(b):
            fc = keep.tile([P, 2 * D], U32, name="fc", align_bytes=64)
            fs = keep.tile([P, 2 * D], U8, name="fs", align_bytes=64)
            nc.vector.quantize_mx(
                out=fc[:].bitcast(FP8X4),
                scales=fs[:],
                in_=st[("fg", b)][:].rearrange("p g d t -> p (g d t)"),
            )
            st[("fc", b)] = (fc, fs)

        def vh_of(b):
            return VH.get(b, VHD)

        def rowsum(b, j):
            a_row = st[("a", b, j // 2)][:, j % 2, :]
            if j == 0:
                deg_new = small.tile([P, 8], F32, name="deg")
                st[("deg", b)] = deg_new
                if vh_of(b):
                    degv_new = small.tile([P, 8], F32, name="degv")
                    st[("degv", b)] = degv_new
            if j in vh_of(b):
                nc.vector.scalar_tensor_tensor(
                    out=junkv[:],
                    in0=a_row[:, 0 : N // 2],
                    scalar=1.0,
                    in1=a_row[:, N // 2 : N],
                    op0=ALU.mult,
                    op1=ALU.add,
                    accum_out=st[("degv", b)][:, j : j + 1],
                )
            else:
                nc.scalar.activation(
                    out=junk[:], in_=a_row, func=ACT.Copy, accum_out=st[("deg", b)][:, j : j + 1]
                )

        def runs(b):
            res = []
            for j in range(8):
                key = "degv" if j in vh_of(b) else "deg"
                if res and res[-1][0] == key:
                    res[-1][2] = j + 1
                else:
                    res.append([key, j, j + 1])
            return res

        def root(b):
            rt = small.tile([P, 8], F32, name="rt")
            for key, j0, j1 in runs(b):
                nc.scalar.activation(out=rt[:, j0:j1], in_=st[(key, b)][:, j0:j1], func=ACT.Sqrt)
            st[("rt", b)] = rt

        def rvec(b):
            rtc = small.tile([P, 8], F32, name="rtc")
            nc.vector.tensor_scalar_max(out=rtc[:], in0=st[("rt", b)][:], scalar1=1e-30)
            inv = small.tile([P, 8], F32, name="inv")
            nc.vector.reciprocal(out=inv[:], in_=rtc[:])
            r = small.tile([P, 8], F32, name="r")
            for key, j0, j1 in runs(b):
                nc.vector.scalar_tensor_tensor(
                    out=r[:, j0:j1],
                    in0=st[(key, b)][:, j0:j1],
                    scalar=0.0,
                    in1=inv[:, j0:j1],
                    op0=ALU.is_gt,
                    op1=ALU.mult,
                )
            st[("r", b)] = r

        def prescale(b, j):
            t1 = tpool.tile([P, N], F32, name="t1")
            who = PSW.get(b, PSWD)[j]
            src = st[("a", b, j // 2)][:, j % 2, :]
            sc = st[("r", b)][:, j : j + 1]
            if who == "G":
                nc.gpsimd.tensor_scalar(
                    out=t1[:], in0=src, scalar1=sc, scalar2=0.0, op0=ALU.mult, op1=ALU.add
                )
            elif who == "V":
                nc.vector.tensor_scalar_mul(out=t1[:], in0=src, scalar1=sc)
            else:
                nc.scalar.activation(out=t1[:], in_=src, func=ACT.Copy, scale=sc)
            st[("t1", b, j)] = t1

        def a_transpose(b, j, g):
            tp = psum.tile([P, 4, P], F32, name="tp", tag="w", bufs=W_BUFS)
            t1 = st[("t1", b, j)]
            for t in range(4):
                c0 = 512 * g + P * t
                nc.tensor.transpose(tp[:, t, :], t1[:, c0 : c0 + P], ident_f[:])
            st[("tp", b, j, g)] = tp

        def a_scale(b, j, g):
            if g == 0:
                gq_new = qpool.tile([P, 2, P, 4], BF16, name="gq", align_bytes=64)
                st[("gq", b, j)] = gq_new
            nc.vector.tensor_tensor(
                out=st[("gq", b, j)][:, g, :, :],
                in0=st[("tp", b, j, g)][:].rearrange("p t n -> p n t"),
                in1=st[("r", b)][:, 4 * g : 4 * g + 4].unsqueeze(1).to_broadcast([P, P, 4]),
                op=ALU.mult,
            )

        def a_quant(b, j):
            ac = cpool.tile([P, 2 * P], U32, name="ac", align_bytes=64)
            asc = cpool.tile([P, 2 * P], U8, name="asc", align_bytes=64)
            nc.vector.quantize_mx(
                out=ac[:].bitcast(FP8X4),
                scales=asc[:],
                in_=st[("gq", b, j)][:].rearrange("p g n t -> p (g n t)"),
            )
            st[("ac", b, j)] = (ac, asc)

        def mx(b, j):
            ac, asc = st[("ac", b, j)]
            fc, fs = st[("fc", b)]
            if j % 2 == 0:
                op_new = psum.tile([P, 2, D], F32, name="op", tag="o", bufs=2)
                st[("op", b, j // 2)] = op_new
            op = st[("op", b, j // 2)]
            for k in range(3):
                nc.tensor.matmul_mx(
                    out=op[:, j % 2, :],
                    lhsT=fc[:, 0:P].bitcast(FP8X4),
                    lhsT_scale=fs[:, 0:P],
                    rhs=fc[:, D : 2 * D].bitcast(FP8X4),
                    rhs_scale=fs[:, D : 2 * D],
                    start=True,
                    stop=True,
                )
            for g in range(2):
                nc.tensor.matmul_mx(
                    out=op[:, j % 2, :],
                    lhsT=ac[:, g * P : (g + 1) * P].bitcast(FP8X4),
                    lhsT_scale=asc[:, g * P : (g + 1) * P],
                    rhs=fc[:, g * D : (g + 1) * D].bitcast(FP8X4),
                    rhs_scale=fs[:, g * D : (g + 1) * D],
                    start=(g == 0),
                    stop=(g == 1),
                )

        def relu_store(b, c):
            ov = out[b].rearrange("(j p) d -> p j d", p=P)
            o_sb = opool.tile([P, 2, D], F32, name="o_sb")
            nc.scalar.activation(out=o_sb[:], in_=st[("op", b, c)][:], func=ACT.Relu)
            nc.scalar.dma_start(out=ov[:, 2 * c : 2 * c + 2, :], in_=o_sb[:])

        lx = -1000.0
        first = set()
        for kind, i, c in FIRST_LOADS:
            lx += 0.01
            if kind == "x":
                at(lx, lambda i=i: load_x(i))
            else:
                first.add((i, c))
                at(lx, lambda i=i, c=c: load_a(i, c))
        for b in range(B):
            for c in range(4):
                if (b, c) not in first:
                    at(8 * b + 2 * c - LLA, lambda b=b, c=c: load_a(b, c))
            xr = 8 * b - LPS - LRV - LSQ
            for j in range(8):
                at(xr - (7 - j) * DRS, lambda b=b, j=j: rowsum(b, j))
            at(xr + 0.01, lambda b=b: root(b))
            at(xr + LSQ, lambda b=b: rvec(b))
            for j in range(8):
                i = 8 * b + j
                at(i - LPS, lambda b=b, j=j: prescale(b, j))
                for g in range(2):
                    at(i - LW + 0.4 * g, lambda b=b, j=j, g=g: a_transpose(b, j, g))
                    at(i + 0.4 * g, lambda b=b, j=j, g=g: a_scale(b, j, g))
                at(i + LQ, lambda b=b, j=j: a_quant(b, j))
                at(i + LQ + LMX, lambda b=b, j=j: mx(b, j))
                if j % 2 == 1:
                    at(i + LQ + LMX + LRL, lambda b=b, j=j: relu_store(b, j // 2))
            x0 = XF0 + b * DXF
            at(x0, lambda b=b: x_transpose(b))
            at(x0 + 1.0, lambda b=b: x_copy(b))
            for i in range(4):
                at(x0 + LFM + i * DF, lambda b=b, i=i: f_matmul(b, i))
                at(x0 + LFM + i * DF + LFB, lambda b=b, i=i: f_bias(b, i))
            at(x0 + LFM + 3 * DF + LFB + LQF, lambda b=b: f_quant(b))
        for item in sorted(plan, key=lambda it: (it[0], it[1])):
            item[2]()
